import numpy as np
import ml_dtypes


BF16 = ml_dtypes.bfloat16


def bf(x):
    return np.asarray(x, np.float32).astype(BF16)


def f64(x):
    return np.asarray(x).astype(np.float64)


E2M1 = np.array([0.0, 0.5, 1.0, 1.5, 2.0, 3.0, 4.0, 6.0, -0.0, -0.5, -1.0, -1.5, -2.0, -3.0, -4.0, -6.0])


def pack_weight(w, fmt):
    k, n = w.shape
    w = f64(bf(w)).reshape(k // 32, 32, n)
    amax = np.abs(w).max(1)
    if fmt == "e4m3":
        byte = np.frexp(amax)[1] - 1 + 127 - 7
    else:
        mant, ex = np.frexp(amax / 6.0)
        byte = np.where(mant > 0.5, ex, ex - 1) + 127
    byte = np.clip(np.where(amax > 0, byte, 1), 1, 254)
    scaled = (w * np.exp2(127.0 - byte)[:, None, :]).reshape(k, n).astype(np.float32)
    by_word = np.ascontiguousarray(scaled.reshape(k // 512, 128, 4, n).transpose(0, 1, 3, 2))
    if fmt == "e4m3":
        words = by_word.astype(ml_dtypes.float8_e4m3fn).view(np.uint8)
    else:
        c = by_word.astype(ml_dtypes.float4_e2m1fn).view(np.uint8) & 0xF
        words = c[..., 0::2] | (c[..., 1::2] << 4)
    return np.ascontiguousarray(words), np.ascontiguousarray(byte.astype(np.uint8).reshape(k // 512, 16, n))


def unpack_weight(words, scales, fmt):
    g, p, n, _ = words.shape
    if fmt == "e4m3":
        vals = np.ascontiguousarray(words).view(ml_dtypes.float8_e4m3fn).astype(np.float64)
    else:
        nib = np.empty((g, p, n, 4), np.uint8)
        nib[..., 0::2] = words & 0xF
        nib[..., 1::2] = words >> 4
        vals = E2M1[nib]
    vals = vals * np.repeat(np.exp2(scales.astype(np.float64) - 127.0), 8, axis=1)[..., None]
    return vals.transpose(0, 1, 3, 2).reshape(g * 512, n)

def pack4(w):
    words, scales = pack_weight(w, "e2m1")
    return words.reshape(words.shape[0], 128, -1), scales


def unpack4(words, scales):
    return unpack_weight(words.reshape(words.shape[0], 128, -1, 2), scales, "e2m1")


def kspread(k):
    return np.exp2(np.repeat(np.random.randint(-6, 7, k // 32), 32).astype(np.float64))


B, S, E, H, DH, ROT, MP = 2, 512, 1536, 8, 128, 32, 4
HD = H * DH
LOC = HD // MP


def rope_sincos():
    inv_freq = 1.0 / (10000.0 ** (np.arange(0, ROT, 2) / ROT))
    ang = np.arange(S)[:, None] * inv_freq[None, :]
    return np.sin(ang), np.cos(ang)


def apply_rope(x, sin, cos):
    sin2 = np.repeat(sin, 2, axis=-1)[None, :, None, :]
    cos2 = np.repeat(cos, 2, axis=-1)[None, :, None, :]
    x1 = x[..., ::2]
    x2 = x[..., 1::2]
    rot = np.stack((-x2, x1), axis=-1).reshape(x.shape)
    return x * cos2 + rot * sin2


def setup_inputs():
    s = kspread(E)
    hidden_states = np.random.standard_normal((B, S, E)) * s
    hidden_states_words, hidden_states_scales = pack4(np.ascontiguousarray(hidden_states.reshape(B * S, E).T))
    w = np.random.standard_normal((3 * HD, E)) / np.sqrt(E) / s[None, :]
    words, scales = pack4(np.ascontiguousarray(w.T))
    return {"hidden_states_words": hidden_states_words,
            "hidden_states_scales": hidden_states_scales,
            "W_qkv_words": words,
            "W_qkv_scales": scales}


def reference(hidden_states_words, hidden_states_scales, W_qkv_words, W_qkv_scales):
    hs = unpack4(hidden_states_words, hidden_states_scales).T.reshape(B, S, E)
    qkv = hs @ unpack4(W_qkv_words, W_qkv_scales)
    qkv = qkv.reshape(B, S, MP, 3 * LOC)
    q, k, v = np.split(qkv, 3, axis=-1)
    q = q.reshape(B, S, H, DH)
    k = k.reshape(B, S, H, DH)
    v = v.reshape(B, S, H, DH)
    sin, cos = rope_sincos()
    q = np.concatenate([apply_rope(q[..., :ROT], sin, cos), q[..., ROT:]], axis=-1)
    k = np.concatenate([apply_rope(k[..., :ROT], sin, cos), k[..., ROT:]], axis=-1)
    return q, k, v

@@ -1,0 +1,232 @@
+from contextlib import ExitStack
+import math
+
+import concourse.mybir as mybir
+
+F32 = mybir.dt.float32
+BF16 = mybir.dt.bfloat16
+I32 = mybir.dt.int32
+U8 = mybir.dt.uint8
+FP4X4 = mybir.dt.float4_e2m1fn_x4
+ALU = mybir.AluOpType
+ACT = mybir.ActivationFunctionType
+
+P = 128
+TOKENS = 1024
+K = 1536
+COLS = 3072
+PASSES = K // 512
+FLOPS = 2 * TOKENS * K * COLS
+
+PIECE = 256
+ROT = 32
+HALF_ROT = ROT // 2
+WARM = 5
+RES_BUFS = 24
+
+
+def tile_progenattention_pa_kernel(
+    tc, hidden_states_words, hidden_states_scales, W_qkv_words, W_qkv_scales, out_0, out_1, out_2
+):
+    nc = tc.nc
+    outs = [o.rearrange("b s h d -> (b s) (h d)") for o in (out_0, out_1, out_2)]
+
+    with ExitStack() as ctx:
+        keep = ctx.enter_context(tc.tile_pool(name="keep", bufs=1))
+        res = ctx.enter_context(tc.tile_pool(name="res", bufs=RES_BUFS))
+        tmp = ctx.enter_context(tc.tile_pool(name="tmp", bufs=4))
+        psum = ctx.enter_context(tc.psum_pool(name="psum", bufs=8))
+
+        x_first = [keep.tile([P, 1024], U8, name="x_first%d" % g, align_bytes=64) for g in range(PASSES)]
+        x_rest = keep.tile([P, PASSES, 1024], U8, name="x_rest", align_bytes=64)
+        xs_first = keep.tile([P, PASSES, 512], U8, name="xs_first", align_bytes=64)
+        xs_rest = keep.tile([P, PASSES, 512], U8, name="xs_rest", align_bytes=64)
+        w_first = [keep.tile([P, 1024], U8, name="w_first%d" % g, align_bytes=64) for g in range(PASSES)]
+        w_b1 = keep.tile([P, PASSES, 1024], U8, name="w_b1", align_bytes=64)
+        w_b2 = keep.tile([P, PASSES, 1024], U8, name="w_b2", align_bytes=64)
+        w_rest = keep.tile([P, PASSES, 3072], U8, name="w_rest", align_bytes=64)
+        ws_first = keep.tile([P, PASSES, 512], U8, name="ws_first", align_bytes=64)
+        ws_mid = keep.tile([P, PASSES, 1024], U8, name="ws_mid", align_bytes=64)
+        ws_rest = keep.tile([P, PASSES, 1536], U8, name="ws_rest", align_bytes=64)
+
+        x_codes = [
+            (0, 512, [x_first[g][:] for g in range(PASSES)]),
+            (512, 1024, [x_rest[:, g, :] for g in range(PASSES)]),
+        ]
+        x_planes = [(0, 512, xs_first), (512, 1024, xs_rest)]
+        w_codes = [
+            (0, 512, [w_first[g][:] for g in range(PASSES)]),
+            (512, 1024, [w_b1[:, g, :] for g in range(PASSES)]),
+            (1024, 1536, [w_b2[:, g, :] for g in range(PASSES)]),
+            (1536, 3072, [w_rest[:, g, :] for g in range(PASSES)]),
+        ]
+        w_planes = [(0, 512, ws_first), (512, 1536, ws_mid), (1536, 3072, ws_rest)]
+
+        def operand(codes, planes, c0, n, g):
+            code = None
+            scale = None
+            for a, b, aps in codes:
+                if a <= c0 and c0 + n <= b:
+                    code = aps[g][:, 2 * (c0 - a) : 2 * (c0 - a + n)]
+            for a, b, plane in planes:
+                if a <= c0 and c0 + n <= b:
+                    scale = plane[:, g, c0 - a : c0 - a + n]
+            return code, scale
+
+        def load_scales(plane, src, c0, c1):
+            for quad in range(4):
+                nc.sync.dma_start(
+                    out=plane[32 * quad : 32 * quad + 4, :, :].bitcast(I32),
+                    in_=src[:, 4 * quad : 4 * quad + 4, c0:c1].rearrange("g r n -> r g n").bitcast(I32),
+                )
+
+        def load_codes_all_passes(dst, src, c0, c1):
+            nc.sync.dma_start(
+                out=dst[:].bitcast(I32),
+                in_=src[:, :, 2 * c0 : 2 * c1].rearrange("g p n -> p g n").bitcast(I32),
+            )
+
+        nc.vector.memset(xs_first[:].bitcast(I32), 0)
+        nc.vector.memset(ws_first[:].bitcast(I32), 0)
+
+        zeros = keep.tile([P, 512], BF16, name="zeros")
+        nc.gpsimd.memset(zeros[:], 0.0)
+        pos = keep.tile([P, 4], F32, name="pos")
+        nc.gpsimd.iota(pos[:], pattern=[[P, 4]], base=0, channel_multiplier=1, allow_small_or_imprecise_dtypes=True)
+
+        nc.sync.dma_start(out=x_first[0][:].bitcast(I32), in_=hidden_states_words[0, :, 0:1024].bitcast(I32))
+        nc.sync.dma_start(out=w_first[0][:].bitcast(I32), in_=W_qkv_words[0, :, 0:1024].bitcast(I32))
+        load_scales(xs_first, hidden_states_scales, 0, 512)
+        load_scales(ws_first, W_qkv_scales, 0, 512)
+        for g in range(1, PASSES):
+            nc.sync.dma_start(out=x_first[g][:].bitcast(I32), in_=hidden_states_words[g, :, 0:1024].bitcast(I32))
+            nc.sync.dma_start(out=w_first[g][:].bitcast(I32), in_=W_qkv_words[g, :, 0:1024].bitcast(I32))
+
+        nc.vector.memset(ws_mid[:].bitcast(I32), 0)
+        nc.vector.memset(xs_rest[:].bitcast(I32), 0)
+        nc.vector.memset(ws_rest[:].bitcast(I32), 0)
+
+        load_codes_all_passes(w_b1, W_qkv_words, 512, 1024)
+        load_scales(ws_mid, W_qkv_scales, 512, 1536)
+        load_scales(xs_rest, hidden_states_scales, 512, 1024)
+        load_codes_all_passes(w_b2, W_qkv_words, 1024, 1536)
+        load_codes_all_passes(x_rest, hidden_states_words, 512, 1024)
+        load_codes_all_passes(w_rest, W_qkv_words, 1536, 3072)
+        load_scales(ws_rest, W_qkv_scales, 1536, 3072)
+
+        warm = psum.tile([P, 512], F32, name="warm", tag="acc")
+        for i in range(WARM):
+            nc.tensor.matmul(out=warm[:], lhsT=zeros[:, 0:P], rhs=zeros[:], start=True, stop=True)
+
+        one = keep.tile([P, 1], F32, name="one")
+        nc.gpsimd.memset(one[:], 0.0)
+        nc.scalar.activation(out=one[:], in_=one[:], func=ACT.Sin)
+
+        turn = keep.tile([P, 4, 2, HALF_ROT], F32, name="turn")
+        for j in range(HALF_ROT):
+            freq = 1.0 / (10000.0 ** (2.0 * j / ROT))
+            nc.vector.tensor_scalar_mul(out=turn[:, :, 1, j], in0=pos[:], scalar1=freq / (2.0 * math.pi))
+        nc.vector.tensor_scalar_add(out=turn[:, :, 0, :], in0=turn[:, :, 1, :], scalar1=0.25)
+        turn_flat = turn[:].rearrange("p t c j -> p (t c j)")
+        whole_i = keep.tile([P, 128], I32, name="whole_i")
+        nc.vector.tensor_copy(out=whole_i[:], in_=turn_flat)
+        whole_f = keep.tile([P, 128], F32, name="whole_f")
+        nc.vector.tensor_copy(out=whole_f[:], in_=whole_i[:])
+        frac = keep.tile([P, 128], F32, name="frac")
+        nc.vector.tensor_sub(out=frac[:], in0=turn_flat, in1=whole_f[:])
+        neg = keep.tile([P, 128], F32, name="neg")
+        nc.vector.scalar_tensor_tensor(out=neg[:], in0=frac[:], scalar=0.5, in1=frac[:], op0=ALU.is_gt, op1=ALU.subtract)
+        cs = keep.tile([P, 4, 2, HALF_ROT], F32, name="cs")
+        nc.scalar.activation(out=cs[:].rearrange("p t c j -> p (t c j)"), in_=neg[:], func=ACT.Sin, scale=-2.0 * math.pi)
+
+        cos_tab = keep.tile([P, 4, 4, ROT], F32, name="cos_tab")
+        sin_tab = keep.tile([P, 4, 4, ROT], F32, name="sin_tab")
+        cos5 = cos_tab[:].rearrange("p t h (j e) -> p t h j e", e=2)
+        sin5 = sin_tab[:].rearrange("p t h (j e) -> p t h j e", e=2)
+        nc.vector.tensor_copy(out=cos5[:, :, 0, :, 0], in_=cs[:, :, 0, :])
+        nc.vector.tensor_copy(out=cos5[:, :, 0, :, 1], in_=cs[:, :, 0, :])
+        nc.vector.tensor_scalar_mul(out=sin5[:, :, 0, :, 0], in0=cs[:, :, 1, :], scalar1=-1.0)
+        nc.vector.tensor_copy(out=sin5[:, :, 0, :, 1], in_=cs[:, :, 1, :])
+        for tab in (cos_tab, sin_tab):
+            nc.vector.tensor_copy(out=tab[:, :, 1, :], in_=tab[:, :, 0, :])
+            nc.vector.tensor_copy(out=tab[:, :, 2:4, :], in_=tab[:, :, 0:2, :])
+
+        results = {}
+
+        def one_pass(acc, t, c0, n, g):
+            xc, xs = operand(x_codes, x_planes, t * P, P, g)
+            wc, ws = operand(w_codes, w_planes, c0, n, g)
+            nc.tensor.matmul_mx(
+                out=acc,
+                lhsT=xc.bitcast(FP4X4),
+                lhsT_scale=xs,
+                rhs=wc.bitcast(FP4X4),
+                rhs_scale=ws,
+                start=(g == 0),
+                stop=(g == PASSES - 1),
+            )
+
+        def rope(r, t):
+            tp = t % 4
+            x = r[:].rearrange("p (h d) -> p h d", h=4)[:, :, 0:ROT]
+            x_swapped = r[:].rearrange("p (h j e) -> p h j e", h=4, e=2)[:, :, 0:HALF_ROT, ::-1]
+            tb = tmp.tile([P, 4, HALF_ROT, 2], F32, name="tb", tag="tb")
+            ta = tmp.tile([P, 4, ROT], F32, name="ta", tag="ta")
+            nc.vector.tensor_mul(out=tb[:], in0=x_swapped, in1=sin_tab[:, tp, :, :].rearrange("p h (j e) -> p h j e", e=2))
+            nc.vector.tensor_mul(out=ta[:], in0=x, in1=cos_tab[:, tp, :, :])
+            nc.vector.tensor_add(out=x, in0=ta[:], in1=tb[:].rearrange("p h j e -> p h (j e)"))
+
+        def empty(acc, t, c0, n, on_vector, split_v):
+            for i in range(n // PIECE):
+                piece = c0 // PIECE + i
+                grp = piece // 3
+                kind = piece % 3
+                sb = grp // 2
+                key = (t, sb, kind)
+                if key not in results:
+                    results[key] = res.tile([P, 512], F32, name="r%d_%d_%d" % key, tag="res")
+                r = results[key]
+                half = grp % 2
+                dst = r[:, half * PIECE : (half + 1) * PIECE]
+                src = acc[:, i * PIECE : (i + 1) * PIECE]
+                if on_vector:
+                    nc.vector.tensor_copy(out=dst, in_=src)
+                else:
+                    nc.scalar.copy(out=dst, in_=src)
+                rows = slice(t * P, (t + 1) * P)
+                if kind == 2 and split_v:
+                    col = sb * 512 + half * PIECE
+                    nc.sync.dma_start(out=outs[kind][rows, col : col + PIECE], in_=dst)
+                elif half == 1:
+                    if kind < 2:
+                        rope(r, t)
+                    nc.sync.dma_start(out=outs[kind][rows, sb * 512 : (sb + 1) * 512], in_=r[:])
+
+        def group(t, c0, n, on_vector, split_v=False):
+            acc = psum.tile([P, 512], F32, name="acc", tag="acc")
+            for g in range(PASSES):
+                one_pass(acc[:, 0:n], t, c0, n, g)
+            empty(acc, t, c0, n, on_vector, split_v)
+
+        first = [psum.tile([P, 512], F32, name="first%d" % t, tag="acc") for t in range(4)]
+        for g in range(PASSES):
+            for t in range(4):
+                one_pass(first[t][:], t, 0, 512, g)
+        for t in range(4):
+            empty(first[t], t, 0, 512, False, False)
+        for b in (1, 2):
+            for t in range(4):
+                group(t, b * 512, 512, b == 2)
+        for t in range(4, 8):
+            for b in range(3):
+                group(t, b * 512, 512, b == 2)
+        for t in range(6):
+            for b in range(3, 6):
+                group(t, b * 512, 512, b == 5)
+        for t in (6, 7):
+            group(t, 1536, 512, False)
+            group(t, 9 * PIECE, PIECE, False)
+            group(t, 10 * PIECE, PIECE, True)
+        for t in (6, 7):
+            group(t, 8 * PIECE, PIECE, False, True)
+            group(t, 11 * PIECE, PIECE, False, True)

@@ -36,6 +36,7 @@ def tile_progenattention_pa_kernel(
         res = ctx.enter_context(tc.tile_pool(name="res", bufs=RES_BUFS))
         tmp = ctx.enter_context(tc.tile_pool(name="tmp", bufs=4))
         psum = ctx.enter_context(tc.psum_pool(name="psum", bufs=8))
+        ctx.enter_context(tc.manual_schedule(engines={mybir.EngineType.SP}))
 
         x_first = [keep.tile([P, 1024], U8, name="x_first%d" % g, align_bytes=64) for g in range(PASSES)]
         x_rest = keep.tile([P, PASSES, 1024], U8, name="x_rest", align_bytes=64)
@@ -86,33 +87,33 @@ def tile_progenattention_pa_kernel(
                 in_=src[:, :, 2 * c0 : 2 * c1].rearrange("g p n -> p g n").bitcast(I32),
             )
 
-        nc.vector.memset(xs_first[:].bitcast(I32), 0)
+        nc.gpsimd.memset(xs_first[:].bitcast(F32), 0.0)
         nc.vector.memset(ws_first[:].bitcast(I32), 0)
+        nc.vector.memset(ws_mid[:].bitcast(I32), 0)
+        nc.vector.memset(xs_rest[:].bitcast(I32), 0)
+        nc.vector.memset(ws_rest[:].bitcast(I32), 0)
 
         zeros = keep.tile([P, 512], BF16, name="zeros")
         nc.gpsimd.memset(zeros[:], 0.0)
         pos = keep.tile([P, 4], F32, name="pos")
         nc.gpsimd.iota(pos[:], pattern=[[P, 4]], base=0, channel_multiplier=1, allow_small_or_imprecise_dtypes=True)
 
-        nc.sync.dma_start(out=x_first[0][:].bitcast(I32), in_=hidden_states_words[0, :, 0:1024].bitcast(I32))
-        nc.sync.dma_start(out=w_first[0][:].bitcast(I32), in_=W_qkv_words[0, :, 0:1024].bitcast(I32))
-        load_scales(xs_first, hidden_states_scales, 0, 512)
-        load_scales(ws_first, W_qkv_scales, 0, 512)
-        for g in range(1, PASSES):
+        def load_first(g):
             nc.sync.dma_start(out=x_first[g][:].bitcast(I32), in_=hidden_states_words[g, :, 0:1024].bitcast(I32))
             nc.sync.dma_start(out=w_first[g][:].bitcast(I32), in_=W_qkv_words[g, :, 0:1024].bitcast(I32))
 
-        nc.vector.memset(ws_mid[:].bitcast(I32), 0)
-        nc.vector.memset(xs_rest[:].bitcast(I32), 0)
-        nc.vector.memset(ws_rest[:].bitcast(I32), 0)
-
-        load_codes_all_passes(w_b1, W_qkv_words, 512, 1024)
+        load_first(0)
+        load_scales(xs_first, hidden_states_scales, 0, 512)
+        load_scales(ws_first, W_qkv_scales, 0, 512)
+        load_first(1)
         load_scales(ws_mid, W_qkv_scales, 512, 1536)
-        load_scales(xs_rest, hidden_states_scales, 512, 1024)
+        load_first(2)
+        load_codes_all_passes(w_b1, W_qkv_words, 512, 1024)
         load_codes_all_passes(w_b2, W_qkv_words, 1024, 1536)
         load_codes_all_passes(x_rest, hidden_states_words, 512, 1024)
-        load_codes_all_passes(w_rest, W_qkv_words, 1536, 3072)
+        load_scales(xs_rest, hidden_states_scales, 512, 1024)
         load_scales(ws_rest, W_qkv_scales, 1536, 3072)
+        load_codes_all_passes(w_rest, W_qkv_words, 1536, 3072)
 
         warm = psum.tile([P, 512], F32, name="warm", tag="acc")
         for i in range(WARM):
@@ -220,13 +221,13 @@ def tile_progenattention_pa_kernel(
         for t in range(4, 8):
             for b in range(3):
                 group(t, b * 512, 512, b == 2)
-        for t in range(6):
+        for t in range(5):
             for b in range(3, 6):
                 group(t, b * 512, 512, b == 5)
-        for t in (6, 7):
+        for t in (5, 6, 7):
             group(t, 1536, 512, False)
             group(t, 9 * PIECE, PIECE, False)
             group(t, 10 * PIECE, PIECE, True)
-        for t in (6, 7):
+        for t in (5, 6, 7):
             group(t, 8 * PIECE, PIECE, False, True)
-            group(t, 11 * PIECE, PIECE, False, True)
+            group(t, 11 * PIECE, PIECE, True, True)

@@ -23,6 +23,7 @@ ROT = 32
 HALF_ROT = ROT // 2
 WARM = 5
 RES_BUFS = 24
+EARLY = 2
 
 
 def tile_progenattention_pa_kernel(
@@ -30,97 +31,132 @@ def tile_progenattention_pa_kernel(
 ):
     nc = tc.nc
     outs = [o.rearrange("b s h d -> (b s) (h d)") for o in (out_0, out_1, out_2)]
+    xw, xsc, ww, wsc = hidden_states_words, hidden_states_scales, W_qkv_words, W_qkv_scales
 
     with ExitStack() as ctx:
         keep = ctx.enter_context(tc.tile_pool(name="keep", bufs=1))
         res = ctx.enter_context(tc.tile_pool(name="res", bufs=RES_BUFS))
         tmp = ctx.enter_context(tc.tile_pool(name="tmp", bufs=4))
-        psum = ctx.enter_context(tc.psum_pool(name="psum", bufs=8))
-        ctx.enter_context(tc.manual_schedule(engines={mybir.EngineType.SP}))
+        psum = ctx.enter_context(tc.psum_pool(name="psum", bufs=8 - EARLY))
+        psum_e = ctx.enter_context(tc.psum_pool(name="psum_e", bufs=EARLY))
+        ctx.enter_context(tc.manual_schedule(engines={mybir.EngineType.SP, mybir.EngineType.Pool, mybir.EngineType.PE}))
 
-        x_first = [keep.tile([P, 1024], U8, name="x_first%d" % g, align_bytes=64) for g in range(PASSES)]
-        x_rest = keep.tile([P, PASSES, 1024], U8, name="x_rest", align_bytes=64)
-        xs_first = keep.tile([P, PASSES, 512], U8, name="xs_first", align_bytes=64)
-        xs_rest = keep.tile([P, PASSES, 512], U8, name="xs_rest", align_bytes=64)
-        w_first = [keep.tile([P, 1024], U8, name="w_first%d" % g, align_bytes=64) for g in range(PASSES)]
-        w_b1 = keep.tile([P, PASSES, 1024], U8, name="w_b1", align_bytes=64)
-        w_b2 = keep.tile([P, PASSES, 1024], U8, name="w_b2", align_bytes=64)
-        w_rest = keep.tile([P, PASSES, 3072], U8, name="w_rest", align_bytes=64)
-        ws_first = keep.tile([P, PASSES, 512], U8, name="ws_first", align_bytes=64)
-        ws_mid = keep.tile([P, PASSES, 1024], U8, name="ws_mid", align_bytes=64)
-        ws_rest = keep.tile([P, PASSES, 1536], U8, name="ws_rest", align_bytes=64)
+        def u8(name, shape):
+            return keep.tile(shape, U8, name=name, align_bytes=64)
 
-        x_codes = [
-            (0, 512, [x_first[g][:] for g in range(PASSES)]),
-            (512, 1024, [x_rest[:, g, :] for g in range(PASSES)]),
-        ]
-        x_planes = [(0, 512, xs_first), (512, 1024, xs_rest)]
-        w_codes = [
-            (0, 512, [w_first[g][:] for g in range(PASSES)]),
-            (512, 1024, [w_b1[:, g, :] for g in range(PASSES)]),
-            (1024, 1536, [w_b2[:, g, :] for g in range(PASSES)]),
-            (1536, 3072, [w_rest[:, g, :] for g in range(PASSES)]),
-        ]
-        w_planes = [(0, 512, ws_first), (512, 1536, ws_mid), (1536, 3072, ws_rest)]
+        x_a = u8("x_a", [P, PASSES, 256 * EARLY])
+        x_b = u8("x_b", [P, PASSES, 256 * (4 - EARLY)])
+        x_c = u8("x_c", [P, PASSES, 1024])
+        xs_early = u8("xs_early", [P, PASSES, 512])
+        xs_full = u8("xs_full", [P, PASSES, 512])
+        xs_rest = u8("xs_rest", [P, PASSES, 512])
+        w_0 = u8("w_0", [P, PASSES, 1024])
+        w_b1 = u8("w_b1", [P, PASSES, 1024])
+        w_b2 = u8("w_b2", [P, PASSES, 1024])
+        w_rest = u8("w_rest", [P, PASSES, 3072])
+        ws_early = u8("ws_early", [P, PASSES, 512])
+        ws_full = u8("ws_full", [P, PASSES, 512])
+        ws_mid = u8("ws_mid", [P, PASSES, 1024])
+        ws_rest = u8("ws_rest", [P, PASSES, 1536])
+        lx_c = u8("lx_c", [P, 256 * EARLY])
+        lx_s = u8("lx_s", [P, P * EARLY])
+        lw_c = u8("lw_c", [P, 1024])
+        lw_s = u8("lw_s", [P, 512])
 
-        def operand(codes, planes, c0, n, g):
-            code = None
-            scale = None
-            for a, b, aps in codes:
-                if a <= c0 and c0 + n <= b:
-                    code = aps[g][:, 2 * (c0 - a) : 2 * (c0 - a + n)]
-            for a, b, plane in planes:
-                if a <= c0 and c0 + n <= b:
-                    scale = plane[:, g, c0 - a : c0 - a + n]
+        def x_operand(t, g, early):
+            if t < EARLY:
+                code = x_a[:, g, 256 * t : 256 * (t + 1)]
+            elif t < 4:
+                code = x_b[:, g, 256 * (t - EARLY) : 256 * (t - EARLY + 1)]
+            else:
+                code = x_c[:, g, 256 * (t - 4) : 256 * (t - 3)]
+            if early:
+                scale = xs_early[:, g, P * t : P * (t + 1)]
+            elif t < 4:
+                scale = xs_full[:, g, P * t : P * (t + 1)]
+            else:
+                scale = xs_rest[:, g, P * (t - 4) : P * (t - 3)]
             return code, scale
 
-        def load_scales(plane, src, c0, c1):
-            for quad in range(4):
+        def w_operand(c0, n, g, early):
+            for a, b, codes, plane in (
+                (0, 512, w_0, ws_early if early else ws_full),
+                (512, 1024, w_b1, None),
+                (1024, 1536, w_b2, None),
+                (1536, 3072, w_rest, ws_rest),
+            ):
+                if a <= c0 and c0 + n <= b:
+                    code = codes[:, g, 2 * (c0 - a) : 2 * (c0 - a + n)]
+                    if plane is None:
+                        scale = ws_mid[:, g, c0 - 512 : c0 - 512 + n]
+                    else:
+                        scale = plane[:, g, c0 - a : c0 - a + n]
+            return code, scale
+
+        def load_scales(plane, src, c0, c1, quads):
+            for quad in quads:
                 nc.sync.dma_start(
                     out=plane[32 * quad : 32 * quad + 4, :, :].bitcast(I32),
                     in_=src[:, 4 * quad : 4 * quad + 4, c0:c1].rearrange("g r n -> r g n").bitcast(I32),
                 )
 
-        def load_codes_all_passes(dst, src, c0, c1):
+        def load_codes(dst, src, c0, c1):
             nc.sync.dma_start(
                 out=dst[:].bitcast(I32),
                 in_=src[:, :, 2 * c0 : 2 * c1].rearrange("g p n -> p g n").bitcast(I32),
             )
 
-        nc.gpsimd.memset(xs_first[:].bitcast(F32), 0.0)
-        nc.vector.memset(ws_first[:].bitcast(I32), 0)
-        nc.vector.memset(ws_mid[:].bitcast(I32), 0)
-        nc.vector.memset(xs_rest[:].bitcast(I32), 0)
-        nc.vector.memset(ws_rest[:].bitcast(I32), 0)
+        def zero(ap):
+            nc.vector.memset(ap.bitcast(I32), 0)
 
+        def move(dst, src):
+            nc.vector.tensor_copy(out=dst.bitcast(I32), in_=src.bitcast(I32))
+
+        nc.gpsimd.memset(xs_early[:].bitcast(F32), 0.0)
         zeros = keep.tile([P, 512], BF16, name="zeros")
-        nc.gpsimd.memset(zeros[:], 0.0)
+        nc.vector.memset(zeros[:], 0.0)
         pos = keep.tile([P, 4], F32, name="pos")
         nc.gpsimd.iota(pos[:], pattern=[[P, 4]], base=0, channel_multiplier=1, allow_small_or_imprecise_dtypes=True)
+        one = keep.tile([P, 1], F32, name="one")
+        nc.gpsimd.memset(one[:], 0.0)
 
-        def load_first(g):
-            nc.sync.dma_start(out=x_first[g][:].bitcast(I32), in_=hidden_states_words[g, :, 0:1024].bitcast(I32))
-            nc.sync.dma_start(out=w_first[g][:].bitcast(I32), in_=W_qkv_words[g, :, 0:1024].bitcast(I32))
+        zero(ws_early[:])
+        zero(xs_full[96:128, :, :])
+        zero(ws_full[96:128, :, :])
+        zero(xs_rest[:])
+        zero(ws_mid[:])
+        zero(lx_s[:])
+        zero(lw_s[:])
+        zero(lx_c[64:96, :])
+        zero(lw_c[64:96, :])
 
-        load_first(0)
-        load_scales(xs_first, hidden_states_scales, 0, 512)
-        load_scales(ws_first, W_qkv_scales, 0, 512)
-        load_first(1)
-        load_scales(ws_mid, W_qkv_scales, 512, 1536)
-        load_first(2)
-        load_codes_all_passes(w_b1, W_qkv_words, 512, 1024)
-        load_codes_all_passes(w_b2, W_qkv_words, 1024, 1536)
-        load_codes_all_passes(x_rest, hidden_states_words, 512, 1024)
-        load_scales(xs_rest, hidden_states_scales, 512, 1024)
-        load_scales(ws_rest, W_qkv_scales, 1536, 3072)
-        load_codes_all_passes(w_rest, W_qkv_words, 1536, 3072)
+        load_codes(x_a, xw, 0, P * EARLY)
+        load_scales(xs_early, xsc, 0, 512, (0, 1, 2))
+        load_codes(w_0, ww, 0, 512)
+        load_scales(ws_early, wsc, 0, 512, (0, 1, 2))
+        load_scales(xs_full, xsc, 0, 512, (3,))
+        load_scales(ws_full, wsc, 0, 512, (3,))
+        load_codes(x_b, xw, P * EARLY, 512)
+        load_codes(x_c, xw, 512, 1024)
+        load_scales(xs_rest, xsc, 512, 1024, (0, 1, 2, 3))
+        load_scales(ws_mid, wsc, 512, 1536, (0, 1, 2, 3))
+        load_codes(w_b1, ww, 512, 1024)
+        load_codes(w_b2, ww, 1024, 1536)
+        for slot, g in ((0, 1), (1, 2)):
+            rows = slice(32 * slot, 32 * slot + 32)
+            nc.sync.dma_start(out=lx_c[rows, :].bitcast(I32), in_=xw[g, 96:128, 0 : 256 * EARLY].bitcast(I32))
+            nc.sync.dma_start(out=lw_c[rows, :].bitcast(I32), in_=ww[g, 96:128, 0:1024].bitcast(I32))
+            rows = slice(32 * slot, 32 * slot + 4)
+            nc.sync.dma_start(out=lx_s[rows, :].bitcast(I32), in_=xsc[g, 12:16, 0 : P * EARLY].bitcast(I32))
+            nc.sync.dma_start(out=lw_s[rows, :].bitcast(I32), in_=wsc[g, 12:16, 0:512].bitcast(I32))
 
         warm = psum.tile([P, 512], F32, name="warm", tag="acc")
         for i in range(WARM):
             nc.tensor.matmul(out=warm[:], lhsT=zeros[:, 0:P], rhs=zeros[:], start=True, stop=True)
 
-        one = keep.tile([P, 1], F32, name="one")
-        nc.gpsimd.memset(one[:], 0.0)
+        move(xs_full[0:96, :, :], xs_early[0:96, :, :])
+        move(ws_full[0:96, :, :], ws_early[0:96, :, :])
+
         nc.scalar.activation(out=one[:], in_=one[:], func=ACT.Sin)
 
         turn = keep.tile([P, 4, 2, HALF_ROT], F32, name="turn")
@@ -152,20 +188,23 @@ def tile_progenattention_pa_kernel(
             nc.vector.tensor_copy(out=tab[:, :, 1, :], in_=tab[:, :, 0, :])
             nc.vector.tensor_copy(out=tab[:, :, 2:4, :], in_=tab[:, :, 0:2, :])
 
+        move(lx_c[96:128, :], x_a[96:128, 0, :])
+        move(lw_c[96:128, :], w_0[96:128, 0, :])
+        move(lx_s[96:128, :], xs_full[96:128, 0, 0 : P * EARLY])
+        move(lw_s[96:128, :], ws_full[96:128, 0, :])
+        zero(ws_rest[:])
+
         results = {}
 
-        def one_pass(acc, t, c0, n, g):
-            xc, xs = operand(x_codes, x_planes, t * P, P, g)
-            wc, ws = operand(w_codes, w_planes, c0, n, g)
+        def mx(acc, xc, xs, wc, ws, start, stop):
             nc.tensor.matmul_mx(
-                out=acc,
-                lhsT=xc.bitcast(FP4X4),
-                lhsT_scale=xs,
-                rhs=wc.bitcast(FP4X4),
-                rhs_scale=ws,
-                start=(g == 0),
-                stop=(g == PASSES - 1),
+                out=acc, lhsT=xc.bitcast(FP4X4), lhsT_scale=xs, rhs=wc.bitcast(FP4X4), rhs_scale=ws, start=start, stop=stop
             )
+
+        def one_pass(acc, t, c0, n, g, early=False):
+            xc, xs = x_operand(t, g, early)
+            wc, ws = w_operand(c0, n, g, early)
+            mx(acc, xc, xs, wc, ws, g == 0, g == PASSES - 1 and not early)
 
         def rope(r, t):
             tp = t % 4
@@ -185,8 +224,9 @@ def tile_progenattention_pa_kernel(
                 sb = grp // 2
                 key = (t, sb, kind)
                 if key not in results:
-                    results[key] = res.tile([P, 512], F32, name="r%d_%d_%d" % key, tag="res")
-                r = results[key]
+                    results[key] = [res.tile([P, 512], F32, name="r%d_%d_%d" % key, tag="res"), 0]
+                r = results[key][0]
+                results[key][1] += 1
                 half = grp % 2
                 dst = r[:, half * PIECE : (half + 1) * PIECE]
                 src = acc[:, i * PIECE : (i + 1) * PIECE]
@@ -198,7 +238,7 @@ def tile_progenattention_pa_kernel(
                 if kind == 2 and split_v:
                     col = sb * 512 + half * PIECE
                     nc.sync.dma_start(out=outs[kind][rows, col : col + PIECE], in_=dst)
-                elif half == 1:
+                elif results[key][1] == 2:
                     if kind < 2:
                         rope(r, t)
                     nc.sync.dma_start(out=outs[kind][rows, sb * 512 : (sb + 1) * 512], in_=r[:])
@@ -209,17 +249,22 @@ def tile_progenattention_pa_kernel(
                 one_pass(acc[:, 0:n], t, c0, n, g)
             empty(acc, t, c0, n, on_vector, split_v)
 
-        first = [psum.tile([P, 512], F32, name="first%d" % t, tag="acc") for t in range(4)]
+        early_acc = [psum_e.tile([P, 512], F32, name="early%d" % t, tag="early") for t in range(EARLY)]
         for g in range(PASSES):
-            for t in range(4):
-                one_pass(first[t][:], t, 0, 512, g)
-        for t in range(4):
-            empty(first[t], t, 0, 512, False, False)
-        for b in (1, 2):
-            for t in range(4):
+            for t in range(EARLY):
+                one_pass(early_acc[t][:], t, 0, 512, g, True)
+        for t in range(EARLY, 8):
+            group(t, 0, 512, t % 2 == 1)
+        for t in (2, 3):
+            for b in (1, 2):
                 group(t, b * 512, 512, b == 2)
-        for t in range(4, 8):
-            for b in range(3):
+        for t in range(EARLY):
+            mx(early_acc[t][:], lx_c[:, 256 * t : 256 * (t + 1)], lx_s[:, P * t : P * (t + 1)], lw_c[:], lw_s[:], False, True)
+            empty(early_acc[t], t, 0, 512, t % 2 == 1, False)
+        load_scales(ws_rest, wsc, 1536, 3072, (0, 1, 2, 3))
+        load_codes(w_rest, ww, 1536, 3072)
+        for t in (0, 1, 4, 5, 6, 7):
+            for b in (1, 2):
                 group(t, b * 512, 512, b == 2)
         for t in range(5):
             for b in range(3, 6):

@@ -112,9 +112,9 @@ def tile_progenattention_pa_kernel(
         def move(dst, src):
             nc.vector.tensor_copy(out=dst.bitcast(I32), in_=src.bitcast(I32))
 
-        nc.gpsimd.memset(xs_early[:].bitcast(F32), 0.0)
         zeros = keep.tile([P, 512], BF16, name="zeros")
         nc.vector.memset(zeros[:], 0.0)
+        zero(xs_early[:])
         pos = keep.tile([P, 4], F32, name="pos")
         nc.gpsimd.iota(pos[:], pattern=[[P, 4]], base=0, channel_multiplier=1, allow_small_or_imprecise_dtypes=True)
         one = keep.tile([P, 1], F32, name="one")

@@ -22,7 +22,10 @@ PIECE = 256
 ROT = 32
 HALF_ROT = ROT // 2
 WARM = 5
-RES_BUFS = 24
+QK_BUFS = 12
+V_BUFS = 8
+TAIL = 8
+LAG = 2
 EARLY = 2
 
 
@@ -35,7 +38,8 @@ def tile_progenattention_pa_kernel(
 
     with ExitStack() as ctx:
         keep = ctx.enter_context(tc.tile_pool(name="keep", bufs=1))
-        res = ctx.enter_context(tc.tile_pool(name="res", bufs=RES_BUFS))
+        res_qk = ctx.enter_context(tc.tile_pool(name="res_qk", bufs=QK_BUFS))
+        res_v = ctx.enter_context(tc.tile_pool(name="res_v", bufs=V_BUFS))
         tmp = ctx.enter_context(tc.tile_pool(name="tmp", bufs=4))
         psum = ctx.enter_context(tc.psum_pool(name="psum", bufs=8 - EARLY))
         psum_e = ctx.enter_context(tc.psum_pool(name="psum_e", bufs=EARLY))
@@ -51,9 +55,10 @@ def tile_progenattention_pa_kernel(
         xs_full = u8("xs_full", [P, PASSES, 512])
         xs_rest = u8("xs_rest", [P, PASSES, 512])
         w_0 = u8("w_0", [P, PASSES, 1024])
-        w_b1 = u8("w_b1", [P, PASSES, 1024])
-        w_b2 = u8("w_b2", [P, PASSES, 1024])
+        w_mid = u8("w_mid", [P, PASSES, 2048])
         w_rest = u8("w_rest", [P, PASSES, 3072])
+        wv_c = [u8("wv_c%d" % h, [P, PASSES, 1024]) for h in range(2)]
+        wv_s = [u8("wv_s%d" % h, [P, PASSES, 512]) for h in range(2)]
         ws_early = u8("ws_early", [P, PASSES, 512])
         ws_full = u8("ws_full", [P, PASSES, 512])
         ws_mid = u8("ws_mid", [P, PASSES, 1024])
@@ -81,16 +86,12 @@ def tile_progenattention_pa_kernel(
         def w_operand(c0, n, g, early):
             for a, b, codes, plane in (
                 (0, 512, w_0, ws_early if early else ws_full),
-                (512, 1024, w_b1, None),
-                (1024, 1536, w_b2, None),
+                (512, 1536, w_mid, ws_mid),
                 (1536, 3072, w_rest, ws_rest),
             ):
                 if a <= c0 and c0 + n <= b:
                     code = codes[:, g, 2 * (c0 - a) : 2 * (c0 - a + n)]
-                    if plane is None:
-                        scale = ws_mid[:, g, c0 - 512 : c0 - 512 + n]
-                    else:
-                        scale = plane[:, g, c0 - a : c0 - a + n]
+                    scale = plane[:, g, c0 - a : c0 - a + n]
             return code, scale
 
         def load_scales(plane, src, c0, c1, quads):
@@ -112,9 +113,9 @@ def tile_progenattention_pa_kernel(
         def move(dst, src):
             nc.vector.tensor_copy(out=dst.bitcast(I32), in_=src.bitcast(I32))
 
+        nc.gpsimd.memset(xs_early[:].bitcast(F32), 0.0)
         zeros = keep.tile([P, 512], BF16, name="zeros")
         nc.vector.memset(zeros[:], 0.0)
-        zero(xs_early[:])
         pos = keep.tile([P, 4], F32, name="pos")
         nc.gpsimd.iota(pos[:], pattern=[[P, 4]], base=0, channel_multiplier=1, allow_small_or_imprecise_dtypes=True)
         one = keep.tile([P, 1], F32, name="one")
@@ -140,8 +141,7 @@ def tile_progenattention_pa_kernel(
         load_codes(x_c, xw, 512, 1024)
         load_scales(xs_rest, xsc, 512, 1024, (0, 1, 2, 3))
         load_scales(ws_mid, wsc, 512, 1536, (0, 1, 2, 3))
-        load_codes(w_b1, ww, 512, 1024)
-        load_codes(w_b2, ww, 1024, 1536)
+        load_codes(w_mid, ww, 512, 1536)
         for slot, g in ((0, 1), (1, 2)):
             rows = slice(32 * slot, 32 * slot + 32)
             nc.sync.dma_start(out=lx_c[rows, :].bitcast(I32), in_=xw[g, 96:128, 0 : 256 * EARLY].bitcast(I32))
@@ -156,6 +156,10 @@ def tile_progenattention_pa_kernel(
 
         move(xs_full[0:96, :, :], xs_early[0:96, :, :])
         move(ws_full[0:96, :, :], ws_early[0:96, :, :])
+
+        zero(ws_rest[:])
+        load_scales(ws_rest, wsc, 1536, 3072, (0, 1, 2, 3))
+        load_codes(w_rest, ww, 1536, 3072)
 
         nc.scalar.activation(out=one[:], in_=one[:], func=ACT.Sin)
 
@@ -176,8 +180,8 @@ def tile_progenattention_pa_kernel(
         cs = keep.tile([P, 4, 2, HALF_ROT], F32, name="cs")
         nc.scalar.activation(out=cs[:].rearrange("p t c j -> p (t c j)"), in_=neg[:], func=ACT.Sin, scale=-2.0 * math.pi)
 
-        cos_tab = keep.tile([P, 4, 4, ROT], F32, name="cos_tab")
-        sin_tab = keep.tile([P, 4, 4, ROT], F32, name="sin_tab")
+        cos_tab = keep.tile([P, 4, 8, ROT], F32, name="cos_tab")
+        sin_tab = keep.tile([P, 4, 8, ROT], F32, name="sin_tab")
         cos5 = cos_tab[:].rearrange("p t h (j e) -> p t h j e", e=2)
         sin5 = sin_tab[:].rearrange("p t h (j e) -> p t h j e", e=2)
         nc.vector.tensor_copy(out=cos5[:, :, 0, :, 0], in_=cs[:, :, 0, :])
@@ -187,12 +191,19 @@ def tile_progenattention_pa_kernel(
         for tab in (cos_tab, sin_tab):
             nc.vector.tensor_copy(out=tab[:, :, 1, :], in_=tab[:, :, 0, :])
             nc.vector.tensor_copy(out=tab[:, :, 2:4, :], in_=tab[:, :, 0:2, :])
+            nc.vector.tensor_copy(out=tab[:, :, 4:8, :], in_=tab[:, :, 0:4, :])
 
         move(lx_c[96:128, :], x_a[96:128, 0, :])
         move(lw_c[96:128, :], w_0[96:128, 0, :])
         move(lx_s[96:128, :], xs_full[96:128, 0, 0 : P * EARLY])
         move(lw_s[96:128, :], ws_full[96:128, 0, :])
-        zero(ws_rest[:])
+
+        def gather_values(h, codes, plane, first, second):
+            for i, c in enumerate((first, second)):
+                move(wv_c[h][:, :, 512 * i : 512 * (i + 1)], codes[:, :, 2 * c : 2 * c + 512])
+                move(wv_s[h][:, :, PIECE * i : PIECE * (i + 1)], plane[:, :, c : c + PIECE])
+
+        gather_values(0, w_mid, ws_mid, 0, 768)
 
         results = {}
 
@@ -201,78 +212,116 @@ def tile_progenattention_pa_kernel(
                 out=acc, lhsT=xc.bitcast(FP4X4), lhsT_scale=xs, rhs=wc.bitcast(FP4X4), rhs_scale=ws, start=start, stop=stop
             )
 
-        def one_pass(acc, t, c0, n, g, early=False):
-            xc, xs = x_operand(t, g, early)
-            wc, ws = w_operand(c0, n, g, early)
-            mx(acc, xc, xs, wc, ws, g == 0, g == PASSES - 1 and not early)
+        def passes(acc, t, h, strip, early=False):
+            for g in range(PASSES):
+                xc, xs = x_operand(t, g, early)
+                if strip == "v":
+                    wc, ws = wv_c[h][:, g, :], wv_s[h][:, g, :]
+                else:
+                    wc, ws = w_operand(1536 * h + (0 if strip == "a" else 768), 512, g, early)
+                mx(acc, xc, xs, wc, ws, g == 0, g == PASSES - 1 and not early)
 
         def rope(r, t):
             tp = t % 4
-            x = r[:].rearrange("p (h d) -> p h d", h=4)[:, :, 0:ROT]
-            x_swapped = r[:].rearrange("p (h j e) -> p h j e", h=4, e=2)[:, :, 0:HALF_ROT, ::-1]
-            tb = tmp.tile([P, 4, HALF_ROT, 2], F32, name="tb", tag="tb")
-            ta = tmp.tile([P, 4, ROT], F32, name="ta", tag="ta")
+            x = r[:].rearrange("p (h d) -> p h d", h=8)[:, :, 0:ROT]
+            x_swapped = r[:].rearrange("p (h j e) -> p h j e", h=8, e=2)[:, :, 0:HALF_ROT, ::-1]
+            tb = tmp.tile([P, 8, HALF_ROT, 2], F32, name="tb", tag="tb")
+            ta = tmp.tile([P, 8, ROT], F32, name="ta", tag="ta")
             nc.vector.tensor_mul(out=tb[:], in0=x_swapped, in1=sin_tab[:, tp, :, :].rearrange("p h (j e) -> p h j e", e=2))
             nc.vector.tensor_mul(out=ta[:], in0=x, in1=cos_tab[:, tp, :, :])
             nc.vector.tensor_add(out=x, in0=ta[:], in1=tb[:].rearrange("p h j e -> p h (j e)"))
 
-        def empty(acc, t, c0, n, on_vector, split_v):
-            for i in range(n // PIECE):
-                piece = c0 // PIECE + i
-                grp = piece // 3
-                kind = piece % 3
-                sb = grp // 2
-                key = (t, sb, kind)
-                if key not in results:
-                    results[key] = [res.tile([P, 512], F32, name="r%d_%d_%d" % key, tag="res"), 0]
-                r = results[key][0]
-                results[key][1] += 1
-                half = grp % 2
-                dst = r[:, half * PIECE : (half + 1) * PIECE]
-                src = acc[:, i * PIECE : (i + 1) * PIECE]
-                if on_vector:
-                    nc.vector.tensor_copy(out=dst, in_=src)
+        def empty(acc, t, h, strip):
+            rows = slice(t * P, (t + 1) * P)
+            cols = slice(h * 512, (h + 1) * 512)
+            if strip == "v":
+                v = res_v.tile([P, 512], F32, name="v", tag="v")
+                if t % 2 == 1:
+                    nc.vector.tensor_copy(out=v[:], in_=acc[:])
                 else:
-                    nc.scalar.copy(out=dst, in_=src)
-                rows = slice(t * P, (t + 1) * P)
-                if kind == 2 and split_v:
-                    col = sb * 512 + half * PIECE
-                    nc.sync.dma_start(out=outs[kind][rows, col : col + PIECE], in_=dst)
-                elif results[key][1] == 2:
-                    if kind < 2:
-                        rope(r, t)
-                    nc.sync.dma_start(out=outs[kind][rows, sb * 512 : (sb + 1) * 512], in_=r[:])
+                    nc.scalar.copy(out=v[:], in_=acc[:])
+                nc.sync.dma_start(out=outs[2][rows, cols], in_=v[:])
+                return
+            key = (t, h)
+            if key not in results:
+                results[key] = res_qk.tile([P, 1024], F32, name="qk%d_%d" % key, tag="qk")
+            r = results[key]
+            at = 0 if strip == "a" else 1
+            nc.scalar.copy(
+                out=r[:].rearrange("p (s c) -> p s c", c=PIECE)[:, at : at + 3 : 2, :],
+                in_=acc[:].rearrange("p (i c) -> p i c", c=PIECE),
+            )
 
-        def group(t, c0, n, on_vector, split_v=False):
+        waiting = []
+        done = [0]
+        sent = [0]
+
+        def finish(t, h):
+            rope(results[(t, h)], t)
+            waiting.append((done[0] + LAG, t, h))
+
+        def store_rotated(everything=False):
+            for due, t, h in waiting[sent[0] :]:
+                if everything or due <= done[0]:
+                    r = results[(t, h)]
+                    rows = slice(t * P, (t + 1) * P)
+                    cols = slice(h * 512, (h + 1) * 512)
+                    nc.sync.dma_start(out=outs[0][rows, cols], in_=r[:, 0:512])
+                    nc.sync.dma_start(out=outs[1][rows, cols], in_=r[:, 512:1024])
+                    sent[0] += 1
+
+        def group(t, h, strip):
             acc = psum.tile([P, 512], F32, name="acc", tag="acc")
-            for g in range(PASSES):
-                one_pass(acc[:, 0:n], t, c0, n, g)
-            empty(acc, t, c0, n, on_vector, split_v)
+            passes(acc[:], t, h, strip)
+            done[0] += 1
+            store_rotated()
+            empty(acc, t, h, strip)
 
         early_acc = [psum_e.tile([P, 512], F32, name="early%d" % t, tag="early") for t in range(EARLY)]
         for g in range(PASSES):
             for t in range(EARLY):
-                one_pass(early_acc[t][:], t, 0, 512, g, True)
+                xc, xs = x_operand(t, g, True)
+                wc, ws = w_operand(0, 512, g, True)
+                mx(early_acc[t][:], xc, xs, wc, ws, g == 0, False)
         for t in range(EARLY, 8):
-            group(t, 0, 512, t % 2 == 1)
+            group(t, 0, "a")
         for t in (2, 3):
-            for b in (1, 2):
-                group(t, b * 512, 512, b == 2)
+            group(t, 0, "b")
+            finish(t, 0)
         for t in range(EARLY):
             mx(early_acc[t][:], lx_c[:, 256 * t : 256 * (t + 1)], lx_s[:, P * t : P * (t + 1)], lw_c[:], lw_s[:], False, True)
-            empty(early_acc[t], t, 0, 512, t % 2 == 1, False)
-        load_scales(ws_rest, wsc, 1536, 3072, (0, 1, 2, 3))
-        load_codes(w_rest, ww, 1536, 3072)
-        for t in (0, 1, 4, 5, 6, 7):
-            for b in (1, 2):
-                group(t, b * 512, 512, b == 2)
-        for t in range(5):
-            for b in range(3, 6):
-                group(t, b * 512, 512, b == 5)
-        for t in (5, 6, 7):
-            group(t, 1536, 512, False)
-            group(t, 9 * PIECE, PIECE, False)
-            group(t, 10 * PIECE, PIECE, True)
-        for t in (5, 6, 7):
-            group(t, 8 * PIECE, PIECE, False, True)
-            group(t, 11 * PIECE, PIECE, True, True)
+            empty(early_acc[t], t, 0, "a")
+        gather_values(1, w_rest, ws_rest, 512, 1280)
+        for t in (0, 1):
+            group(t, 0, "b")
+            finish(t, 0)
+        for t in (2, 3, 0, 1):
+            group(t, 0, "v")
+        for t in (4, 5, 6, 7):
+            group(t, 0, "b")
+            group(t, 0, "v")
+            finish(t, 0)
+        for t in range(8 - TAIL):
+            group(t, 1, "a")
+            group(t, 1, "b")
+            group(t, 1, "v")
+            finish(t, 1)
+        for t in range(8 - TAIL, 8):
+            group(t, 1, "a")
+            group(t, 1, "b")
+            finish(t, 1)
+        for t in range(8 - TAIL, 7):
+            group(t, 1, "v")
+        store_rotated(True)
+        for i, c0 in enumerate((2048, 2816)):
+            acc = psum.tile([P, 512], F32, name="acc", tag="acc")
+            for g in range(PASSES):
+                xc, xs = x_operand(7, g, False)
+                wc, ws = w_operand(c0, PIECE, g, False)
+                mx(acc[:, 0:PIECE], xc, xs, wc, ws, g == 0, g == PASSES - 1)
+            v = res_v.tile([P, 512], F32, name="v", tag="v")
+            if i == 0:
+                nc.scalar.copy(out=v[:, 0:PIECE], in_=acc[:, 0:PIECE])
+            else:
+                nc.vector.tensor_copy(out=v[:, 0:PIECE], in_=acc[:, 0:PIECE])
+            nc.sync.dma_start(out=outs[2][7 * P : 8 * P, 512 + PIECE * i : 512 + PIECE * (i + 1)], in_=v[:, 0:PIECE])

@@ -132,12 +132,12 @@ def tile_progenattention_pa_kernel(
         zero(lw_c[64:96, :])
 
         load_codes(x_a, xw, 0, P * EARLY)
-        load_scales(xs_early, xsc, 0, 512, (0, 1, 2))
         load_codes(w_0, ww, 0, 512)
+        load_scales(xs_early, xsc, 0, 512, (0, 1, 2))
         load_scales(ws_early, wsc, 0, 512, (0, 1, 2))
+        load_codes(x_b, xw, P * EARLY, 512)
         load_scales(xs_full, xsc, 0, 512, (3,))
         load_scales(ws_full, wsc, 0, 512, (3,))
-        load_codes(x_b, xw, P * EARLY, 512)
         load_codes(x_c, xw, 512, 1024)
         load_scales(xs_rest, xsc, 512, 1024, (0, 1, 2, 3))
         load_scales(ws_mid, wsc, 512, 1536, (0, 1, 2, 3))

@@ -124,10 +124,8 @@ def tile_progenattention_pa_kernel(
         zero(ws_early[:])
         zero(xs_full[96:128, :, :])
         zero(ws_full[96:128, :, :])
-        zero(xs_rest[:])
-        zero(ws_mid[:])
-        zero(lx_s[:])
-        zero(lw_s[:])
+        for plane in (xs_rest, ws_mid, lx_s, lw_s):
+            nc.gpsimd.memset(plane[:].bitcast(F32), 0.0)
         zero(lx_c[64:96, :])
         zero(lw_c[64:96, :])
 
@@ -156,10 +154,6 @@ def tile_progenattention_pa_kernel(
 
         move(xs_full[0:96, :, :], xs_early[0:96, :, :])
         move(ws_full[0:96, :, :], ws_early[0:96, :, :])
-
-        zero(ws_rest[:])
-        load_scales(ws_rest, wsc, 1536, 3072, (0, 1, 2, 3))
-        load_codes(w_rest, ww, 1536, 3072)
 
         nc.scalar.activation(out=one[:], in_=one[:], func=ACT.Sin)
 
@@ -197,6 +191,10 @@ def tile_progenattention_pa_kernel(
         move(lw_c[96:128, :], w_0[96:128, 0, :])
         move(lx_s[96:128, :], xs_full[96:128, 0, 0 : P * EARLY])
         move(lw_s[96:128, :], ws_full[96:128, 0, :])
+
+        zero(ws_rest[:])
+        load_scales(ws_rest, wsc, 1536, 3072, (0, 1, 2, 3))
+        load_codes(w_rest, ww, 1536, 3072)
 
         def gather_values(h, codes, plane, first, second):
             for i, c in enumerate((first, second)):
@@ -320,8 +318,10 @@ def tile_progenattention_pa_kernel(
                 wc, ws = w_operand(c0, PIECE, g, False)
                 mx(acc[:, 0:PIECE], xc, xs, wc, ws, g == 0, g == PASSES - 1)
             v = res_v.tile([P, 512], F32, name="v", tag="v")
+            last = outs[2][7 * P : 8 * P, 512 + PIECE * i : 512 + PIECE * (i + 1)]
             if i == 0:
-                nc.scalar.copy(out=v[:, 0:PIECE], in_=acc[:, 0:PIECE])
-            else:
                 nc.vector.tensor_copy(out=v[:, 0:PIECE], in_=acc[:, 0:PIECE])
-            nc.sync.dma_start(out=outs[2][7 * P : 8 * P, 512 + PIECE * i : 512 + PIECE * (i + 1)], in_=v[:, 0:PIECE])
+                nc.sync.dma_start(out=last, in_=v[:, 0:PIECE])
+            else:
+                nc.scalar.copy(out=v[:, 0:PIECE], in_=acc[:, 0:PIECE])
+                nc.scalar.dma_start(out=last, in_=v[:, 0:PIECE])

@@ -46,7 +46,7 @@ def tile_progenattention_pa_kernel(
         ctx.enter_context(tc.manual_schedule(engines={mybir.EngineType.SP, mybir.EngineType.Pool, mybir.EngineType.PE}))
 
         def u8(name, shape):
-            return keep.tile(shape, U8, name=name, align_bytes=64)
+            return keep.tile(shape, U8, name=name, align_bytes=256)
 
         x_a = u8("x_a", [P, PASSES, 256 * EARLY])
         x_b = u8("x_b", [P, PASSES, 256 * (4 - EARLY)])
@@ -233,7 +233,7 @@ def tile_progenattention_pa_kernel(
             rows = slice(t * P, (t + 1) * P)
             cols = slice(h * 512, (h + 1) * 512)
             if strip == "v":
-                v = res_v.tile([P, 512], F32, name="v", tag="v")
+                v = res_v.tile([P, 512], F32, name="v", tag="v", align_bytes=256)
                 if t % 2 == 1:
                     nc.vector.tensor_copy(out=v[:], in_=acc[:])
                 else:
@@ -242,7 +242,7 @@ def tile_progenattention_pa_kernel(
                 return
             key = (t, h)
             if key not in results:
-                results[key] = res_qk.tile([P, 1024], F32, name="qk%d_%d" % key, tag="qk")
+                results[key] = res_qk.tile([P, 1024], F32, name="qk%d_%d" % key, tag="qk", align_bytes=256)
             r = results[key]
             at = 0 if strip == "a" else 1
             nc.scalar.copy(
@@ -317,7 +317,7 @@ def tile_progenattention_pa_kernel(
                 xc, xs = x_operand(7, g, False)
                 wc, ws = w_operand(c0, PIECE, g, False)
                 mx(acc[:, 0:PIECE], xc, xs, wc, ws, g == 0, g == PASSES - 1)
-            v = res_v.tile([P, 512], F32, name="v", tag="v")
+            v = res_v.tile([P, 512], F32, name="v", tag="v", align_bytes=256)
             last = outs[2][7 * P : 8 * P, 512 + PIECE * i : 512 + PIECE * (i + 1)]
             if i == 0:
                 nc.vector.tensor_copy(out=v[:, 0:PIECE], in_=acc[:, 0:PIECE])

@@ -46,7 +46,7 @@ def tile_progenattention_pa_kernel(
         ctx.enter_context(tc.manual_schedule(engines={mybir.EngineType.SP, mybir.EngineType.Pool, mybir.EngineType.PE}))
 
         def u8(name, shape):
-            return keep.tile(shape, U8, name=name, align_bytes=256)
+            return keep.tile(shape, U8, name=name, align_bytes=1024)
 
         x_a = u8("x_a", [P, PASSES, 256 * EARLY])
         x_b = u8("x_b", [P, PASSES, 256 * (4 - EARLY)])
@@ -233,7 +233,7 @@ def tile_progenattention_pa_kernel(
             rows = slice(t * P, (t + 1) * P)
             cols = slice(h * 512, (h + 1) * 512)
             if strip == "v":
-                v = res_v.tile([P, 512], F32, name="v", tag="v", align_bytes=256)
+                v = res_v.tile([P, 512], F32, name="v", tag="v", align_bytes=2048)
                 if t % 2 == 1:
                     nc.vector.tensor_copy(out=v[:], in_=acc[:])
                 else:
@@ -242,7 +242,7 @@ def tile_progenattention_pa_kernel(
                 return
             key = (t, h)
             if key not in results:
-                results[key] = res_qk.tile([P, 1024], F32, name="qk%d_%d" % key, tag="qk", align_bytes=256)
+                results[key] = res_qk.tile([P, 1024], F32, name="qk%d_%d" % key, tag="qk", align_bytes=4096)
             r = results[key]
             at = 0 if strip == "a" else 1
             nc.scalar.copy(
@@ -317,7 +317,7 @@ def tile_progenattention_pa_kernel(
                 xc, xs = x_operand(7, g, False)
                 wc, ws = w_operand(c0, PIECE, g, False)
                 mx(acc[:, 0:PIECE], xc, xs, wc, ws, g == 0, g == PASSES - 1)
-            v = res_v.tile([P, 512], F32, name="v", tag="v", align_bytes=256)
+            v = res_v.tile([P, 512], F32, name="v", tag="v", align_bytes=2048)
             last = outs[2][7 * P : 8 * P, 512 + PIECE * i : 512 + PIECE * (i + 1)]
             if i == 0:
                 nc.vector.tensor_copy(out=v[:, 0:PIECE], in_=acc[:, 0:PIECE])

from contextlib import ExitStack
import math

import concourse.mybir as mybir

F32 = mybir.dt.float32
BF16 = mybir.dt.bfloat16
I32 = mybir.dt.int32
U8 = mybir.dt.uint8
FP4X4 = mybir.dt.float4_e2m1fn_x4
ALU = mybir.AluOpType
ACT = mybir.ActivationFunctionType

P = 128
TOKENS = 1024
K = 1536
COLS = 3072
PASSES = K // 512
FLOPS = 2 * TOKENS * K * COLS

PIECE = 256
ROT = 32
HALF_ROT = ROT // 2
WARM = 5
QK_BUFS = 12
V_BUFS = 8
TAIL = 8
LAG = 2
EARLY = 2


def tile_progenattention_pa_kernel(
    tc, hidden_states_words, hidden_states_scales, W_qkv_words, W_qkv_scales, out_0, out_1, out_2
):
    nc = tc.nc
    outs = [o.rearrange("b s h d -> (b s) (h d)") for o in (out_0, out_1, out_2)]
    xw, xsc, ww, wsc = hidden_states_words, hidden_states_scales, W_qkv_words, W_qkv_scales

    with ExitStack() as ctx:
        keep = ctx.enter_context(tc.tile_pool(name="keep", bufs=1))
        res_qk = ctx.enter_context(tc.tile_pool(name="res_qk", bufs=QK_BUFS))
        res_v = ctx.enter_context(tc.tile_pool(name="res_v", bufs=V_BUFS))
        tmp = ctx.enter_context(tc.tile_pool(name="tmp", bufs=4))
        psum = ctx.enter_context(tc.psum_pool(name="psum", bufs=8 - EARLY))
        psum_e = ctx.enter_context(tc.psum_pool(name="psum_e", bufs=EARLY))
        ctx.enter_context(tc.manual_schedule(engines={mybir.EngineType.SP, mybir.EngineType.Pool, mybir.EngineType.PE}))

        def u8(name, shape):
            return keep.tile(shape, U8, name=name, align_bytes=1024)

        x_a = u8("x_a", [P, PASSES, 256 * EARLY])
        x_b = u8("x_b", [P, PASSES, 256 * (4 - EARLY)])
        x_c = u8("x_c", [P, PASSES, 1024])
        xs_early = u8("xs_early", [P, PASSES, 512])
        xs_full = u8("xs_full", [P, PASSES, 512])
        xs_rest = u8("xs_rest", [P, PASSES, 512])
        w_0 = u8("w_0", [P, PASSES, 1024])
        w_mid = u8("w_mid", [P, PASSES, 2048])
        w_rest = u8("w_rest", [P, PASSES, 3072])
        wv_c = [u8("wv_c%d" % h, [P, PASSES, 1024]) for h in range(2)]
        wv_s = [u8("wv_s%d" % h, [P, PASSES, 512]) for h in range(2)]
        ws_early = u8("ws_early", [P, PASSES, 512])
        ws_full = u8("ws_full", [P, PASSES, 512])
        ws_mid = u8("ws_mid", [P, PASSES, 1024])
        ws_rest = u8("ws_rest", [P, PASSES, 1536])
        lx_c = u8("lx_c", [P, 256 * EARLY])
        lx_s = u8("lx_s", [P, P * EARLY])
        lw_c = u8("lw_c", [P, 1024])
        lw_s = u8("lw_s", [P, 512])

        def x_operand(t, g, early):
            if t < EARLY:
                code = x_a[:, g, 256 * t : 256 * (t + 1)]
            elif t < 4:
                code = x_b[:, g, 256 * (t - EARLY) : 256 * (t - EARLY + 1)]
            else:
                code = x_c[:, g, 256 * (t - 4) : 256 * (t - 3)]
            if early:
                scale = xs_early[:, g, P * t : P * (t + 1)]
            elif t < 4:
                scale = xs_full[:, g, P * t : P * (t + 1)]
            else:
                scale = xs_rest[:, g, P * (t - 4) : P * (t - 3)]
            return code, scale

        def w_operand(c0, n, g, early):
            for a, b, codes, plane in (
                (0, 512, w_0, ws_early if early else ws_full),
                (512, 1536, w_mid, ws_mid),
                (1536, 3072, w_rest, ws_rest),
            ):
                if a <= c0 and c0 + n <= b:
                    code = codes[:, g, 2 * (c0 - a) : 2 * (c0 - a + n)]
                    scale = plane[:, g, c0 - a : c0 - a + n]
            return code, scale

        def load_scales(plane, src, c0, c1, quads):
            for quad in quads:
                nc.sync.dma_start(
                    out=plane[32 * quad : 32 * quad + 4, :, :].bitcast(I32),
                    in_=src[:, 4 * quad : 4 * quad + 4, c0:c1].rearrange("g r n -> r g n").bitcast(I32),
                )

        def load_codes(dst, src, c0, c1):
            nc.sync.dma_start(
                out=dst[:].bitcast(I32),
                in_=src[:, :, 2 * c0 : 2 * c1].rearrange("g p n -> p g n").bitcast(I32),
            )

        def zero(ap):
            nc.vector.memset(ap.bitcast(I32), 0)

        def move(dst, src):
            nc.vector.tensor_copy(out=dst.bitcast(I32), in_=src.bitcast(I32))

        nc.gpsimd.memset(xs_early[:].bitcast(F32), 0.0)
        zeros = keep.tile([P, 512], BF16, name="zeros")
        nc.vector.memset(zeros[:], 0.0)
        pos = keep.tile([P, 4], F32, name="pos")
        nc.gpsimd.iota(pos[:], pattern=[[P, 4]], base=0, channel_multiplier=1, allow_small_or_imprecise_dtypes=True)
        one = keep.tile([P, 1], F32, name="one")
        nc.gpsimd.memset(one[:], 0.0)

        zero(ws_early[:])
        zero(xs_full[96:128, :, :])
        zero(ws_full[96:128, :, :])
        for plane in (xs_rest, ws_mid, lx_s, lw_s):
            nc.gpsimd.memset(plane[:].bitcast(F32), 0.0)
        zero(lx_c[64:96, :])
        zero(lw_c[64:96, :])

        load_codes(x_a, xw, 0, P * EARLY)
        load_codes(w_0, ww, 0, 512)
        load_scales(xs_early, xsc, 0, 512, (0, 1, 2))
        load_scales(ws_early, wsc, 0, 512, (0, 1, 2))
        load_codes(x_b, xw, P * EARLY, 512)
        load_scales(xs_full, xsc, 0, 512, (3,))
        load_scales(ws_full, wsc, 0, 512, (3,))
        load_codes(x_c, xw, 512, 1024)
        load_scales(xs_rest, xsc, 512, 1024, (0, 1, 2, 3))
        load_scales(ws_mid, wsc, 512, 1536, (0, 1, 2, 3))
        load_codes(w_mid, ww, 512, 1536)
        for slot, g in ((0, 1), (1, 2)):
            rows = slice(32 * slot, 32 * slot + 32)
            nc.sync.dma_start(out=lx_c[rows, :].bitcast(I32), in_=xw[g, 96:128, 0 : 256 * EARLY].bitcast(I32))
            nc.sync.dma_start(out=lw_c[rows, :].bitcast(I32), in_=ww[g, 96:128, 0:1024].bitcast(I32))
            rows = slice(32 * slot, 32 * slot + 4)
            nc.sync.dma_start(out=lx_s[rows, :].bitcast(I32), in_=xsc[g, 12:16, 0 : P * EARLY].bitcast(I32))
            nc.sync.dma_start(out=lw_s[rows, :].bitcast(I32), in_=wsc[g, 12:16, 0:512].bitcast(I32))

        warm = psum.tile([P, 512], F32, name="warm", tag="acc")
        for i in range(WARM):
            nc.tensor.matmul(out=warm[:], lhsT=zeros[:, 0:P], rhs=zeros[:], start=True, stop=True)

        move(xs_full[0:96, :, :], xs_early[0:96, :, :])
        move(ws_full[0:96, :, :], ws_early[0:96, :, :])

        nc.scalar.activation(out=one[:], in_=one[:], func=ACT.Sin)

        turn = keep.tile([P, 4, 2, HALF_ROT], F32, name="turn")
        for j in range(HALF_ROT):
            freq = 1.0 / (10000.0 ** (2.0 * j / ROT))
            nc.vector.tensor_scalar_mul(out=turn[:, :, 1, j], in0=pos[:], scalar1=freq / (2.0 * math.pi))
        nc.vector.tensor_scalar_add(out=turn[:, :, 0, :], in0=turn[:, :, 1, :], scalar1=0.25)
        turn_flat = turn[:].rearrange("p t c j -> p (t c j)")
        whole_i = keep.tile([P, 128], I32, name="whole_i")
        nc.vector.tensor_copy(out=whole_i[:], in_=turn_flat)
        whole_f = keep.tile([P, 128], F32, name="whole_f")
        nc.vector.tensor_copy(out=whole_f[:], in_=whole_i[:])
        frac = keep.tile([P, 128], F32, name="frac")
        nc.vector.tensor_sub(out=frac[:], in0=turn_flat, in1=whole_f[:])
        neg = keep.tile([P, 128], F32, name="neg")
        nc.vector.scalar_tensor_tensor(out=neg[:], in0=frac[:], scalar=0.5, in1=frac[:], op0=ALU.is_gt, op1=ALU.subtract)
        cs = keep.tile([P, 4, 2, HALF_ROT], F32, name="cs")
        nc.scalar.activation(out=cs[:].rearrange("p t c j -> p (t c j)"), in_=neg[:], func=ACT.Sin, scale=-2.0 * math.pi)

        cos_tab = keep.tile([P, 4, 8, ROT], F32, name="cos_tab")
        sin_tab = keep.tile([P, 4, 8, ROT], F32, name="sin_tab")
        cos5 = cos_tab[:].rearrange("p t h (j e) -> p t h j e", e=2)
        sin5 = sin_tab[:].rearrange("p t h (j e) -> p t h j e", e=2)
        nc.vector.tensor_copy(out=cos5[:, :, 0, :, 0], in_=cs[:, :, 0, :])
        nc.vector.tensor_copy(out=cos5[:, :, 0, :, 1], in_=cs[:, :, 0, :])
        nc.vector.tensor_scalar_mul(out=sin5[:, :, 0, :, 0], in0=cs[:, :, 1, :], scalar1=-1.0)
        nc.vector.tensor_copy(out=sin5[:, :, 0, :, 1], in_=cs[:, :, 1, :])
        for tab in (cos_tab, sin_tab):
            nc.vector.tensor_copy(out=tab[:, :, 1, :], in_=tab[:, :, 0, :])
            nc.vector.tensor_copy(out=tab[:, :, 2:4, :], in_=tab[:, :, 0:2, :])
            nc.vector.tensor_copy(out=tab[:, :, 4:8, :], in_=tab[:, :, 0:4, :])

        move(lx_c[96:128, :], x_a[96:128, 0, :])
        move(lw_c[96:128, :], w_0[96:128, 0, :])
        move(lx_s[96:128, :], xs_full[96:128, 0, 0 : P * EARLY])
        move(lw_s[96:128, :], ws_full[96:128, 0, :])

        zero(ws_rest[:])
        load_scales(ws_rest, wsc, 1536, 3072, (0, 1, 2, 3))
        load_codes(w_rest, ww, 1536, 3072)

        def gather_values(h, codes, plane, first, second):
            for i, c in enumerate((first, second)):
                move(wv_c[h][:, :, 512 * i : 512 * (i + 1)], codes[:, :, 2 * c : 2 * c + 512])
                move(wv_s[h][:, :, PIECE * i : PIECE * (i + 1)], plane[:, :, c : c + PIECE])

        gather_values(0, w_mid, ws_mid, 0, 768)

        results = {}

        def mx(acc, xc, xs, wc, ws, start, stop):
            nc.tensor.matmul_mx(
                out=acc, lhsT=xc.bitcast(FP4X4), lhsT_scale=xs, rhs=wc.bitcast(FP4X4), rhs_scale=ws, start=start, stop=stop
            )

        def passes(acc, t, h, strip, early=False):
            for g in range(PASSES):
                xc, xs = x_operand(t, g, early)
                if strip == "v":
                    wc, ws = wv_c[h][:, g, :], wv_s[h][:, g, :]
                else:
                    wc, ws = w_operand(1536 * h + (0 if strip == "a" else 768), 512, g, early)
                mx(acc, xc, xs, wc, ws, g == 0, g == PASSES - 1 and not early)

        def rope(r, t):
            tp = t % 4
            x = r[:].rearrange("p (h d) -> p h d", h=8)[:, :, 0:ROT]
            x_swapped = r[:].rearrange("p (h j e) -> p h j e", h=8, e=2)[:, :, 0:HALF_ROT, ::-1]
            tb = tmp.tile([P, 8, HALF_ROT, 2], F32, name="tb", tag="tb")
            ta = tmp.tile([P, 8, ROT], F32, name="ta", tag="ta")
            nc.vector.tensor_mul(out=tb[:], in0=x_swapped, in1=sin_tab[:, tp, :, :].rearrange("p h (j e) -> p h j e", e=2))
            nc.vector.tensor_mul(out=ta[:], in0=x, in1=cos_tab[:, tp, :, :])
            nc.vector.tensor_add(out=x, in0=ta[:], in1=tb[:].rearrange("p h j e -> p h (j e)"))

        def empty(acc, t, h, strip):
            rows = slice(t * P, (t + 1) * P)
            cols = slice(h * 512, (h + 1) * 512)
            if strip == "v":
                v = res_v.tile([P, 512], F32, name="v", tag="v", align_bytes=2048)
                if t % 2 == 1:
                    nc.vector.tensor_copy(out=v[:], in_=acc[:])
                else:
                    nc.scalar.copy(out=v[:], in_=acc[:])
                nc.sync.dma_start(out=outs[2][rows, cols], in_=v[:])
                return
            key = (t, h)
            if key not in results:
                results[key] = res_qk.tile([P, 1024], F32, name="qk%d_%d" % key, tag="qk", align_bytes=4096)
            r = results[key]
            at = 0 if strip == "a" else 1
            nc.scalar.copy(
                out=r[:].rearrange("p (s c) -> p s c", c=PIECE)[:, at : at + 3 : 2, :],
                in_=acc[:].rearrange("p (i c) -> p i c", c=PIECE),
            )

        waiting = []
        done = [0]
        sent = [0]

        def finish(t, h):
            rope(results[(t, h)], t)
            waiting.append((done[0] + LAG, t, h))

        def store_rotated(everything=False):
            for due, t, h in waiting[sent[0] :]:
                if everything or due <= done[0]:
                    r = results[(t, h)]
                    rows = slice(t * P, (t + 1) * P)
                    cols = slice(h * 512, (h + 1) * 512)
                    nc.sync.dma_start(out=outs[0][rows, cols], in_=r[:, 0:512])
                    nc.sync.dma_start(out=outs[1][rows, cols], in_=r[:, 512:1024])
                    sent[0] += 1

        def group(t, h, strip):
            acc = psum.tile([P, 512], F32, name="acc", tag="acc")
            passes(acc[:], t, h, strip)
            done[0] += 1
            store_rotated()
            empty(acc, t, h, strip)

        early_acc = [psum_e.tile([P, 512], F32, name="early%d" % t, tag="early") for t in range(EARLY)]
        for g in range(PASSES):
            for t in range(EARLY):
                xc, xs = x_operand(t, g, True)
                wc, ws = w_operand(0, 512, g, True)
                mx(early_acc[t][:], xc, xs, wc, ws, g == 0, False)
        for t in range(EARLY, 8):
            group(t, 0, "a")
        for t in (2, 3):
            group(t, 0, "b")
            finish(t, 0)
        for t in range(EARLY):
            mx(early_acc[t][:], lx_c[:, 256 * t : 256 * (t + 1)], lx_s[:, P * t : P * (t + 1)], lw_c[:], lw_s[:], False, True)
            empty(early_acc[t], t, 0, "a")
        gather_values(1, w_rest, ws_rest, 512, 1280)
        for t in (0, 1):
            group(t, 0, "b")
            finish(t, 0)
        for t in (2, 3, 0, 1):
            group(t, 0, "v")
        for t in (4, 5, 6, 7):
            group(t, 0, "b")
            group(t, 0, "v")
            finish(t, 0)
        for t in range(8 - TAIL):
            group(t, 1, "a")
            group(t, 1, "b")
            group(t, 1, "v")
            finish(t, 1)
        for t in range(8 - TAIL, 8):
            group(t, 1, "a")
            group(t, 1, "b")
            finish(t, 1)
        for t in range(8 - TAIL, 7):
            group(t, 1, "v")
        store_rotated(True)
        for i, c0 in enumerate((2048, 2816)):
            acc = psum.tile([P, 512], F32, name="acc", tag="acc")
            for g in range(PASSES):
                xc, xs = x_operand(7, g, False)
                wc, ws = w_operand(c0, PIECE, g, False)
                mx(acc[:, 0:PIECE], xc, xs, wc, ws, g == 0, g == PASSES - 1)
            v = res_v.tile([P, 512], F32, name="v", tag="v", align_bytes=2048)
            last = outs[2][7 * P : 8 * P, 512 + PIECE * i : 512 + PIECE * (i + 1)]
            if i == 0:
                nc.vector.tensor_copy(out=v[:, 0:PIECE], in_=acc[:, 0:PIECE])
                nc.sync.dma_start(out=last, in_=v[:, 0:PIECE])
            else:
                nc.scalar.copy(out=v[:, 0:PIECE], in_=acc[:, 0:PIECE])
                nc.scalar.dma_start(out=last, in_=v[:, 0:PIECE])
